import numpy as np
import ml_dtypes


def mxq(x, axis, fmt="e4m3"):
    dtype, down = {"e4m3": (ml_dtypes.float8_e4m3fn, 7), "e5m2": (ml_dtypes.float8_e5m2, 14)}[fmt]
    v = np.moveaxis(np.asarray(x, np.float32).astype(ml_dtypes.bfloat16).astype(np.float64), axis, -1)
    blocks = v.reshape(v.shape[:-1] + (-1, 32))
    amax = np.abs(blocks).max(-1, keepdims=True)
    byte = np.maximum(np.where(amax > 0, np.frexp(amax)[1] - 1 + 127, 0) - down, 1)
    scale = np.exp2(byte - 127.0)
    codes = (blocks / scale).astype(np.float32).astype(dtype).astype(np.float64)
    return np.moveaxis((codes * scale).reshape(v.shape), -1, axis)


WIDE = False


def mx_kscale(k):
    if not WIDE:
        return np.ones(k)
    levels = np.array([10, -10, 5, -5, 0])
    a = np.random.permutation(np.resize(levels, k // 512 * 4)).reshape(k // 512, 4)
    idx = np.arange(k)
    return np.exp2(a[idx // 512, idx % 128 // 32])


BF16 = ml_dtypes.bfloat16


def bf(x):
    return np.asarray(x, np.float32).astype(BF16)


def f64(x):
    return np.asarray(x).astype(np.float64)


B, C, H, W, O = 2, 128, 64, 64, 128
K = 4 * C


def haar_dwt2(x):
    nb, nc_, nh, nw = x.shape
    xr = x.reshape(nb, nc_, nh // 2, 2, nw // 2, 2)
    a = xr[:, :, :, 0, :, 0]
    b = xr[:, :, :, 0, :, 1]
    c = xr[:, :, :, 1, :, 0]
    d = xr[:, :, :, 1, :, 1]
    half = 0.5
    LL = (a + b + c + d) * half
    LH = (a + b - c - d) * half
    HL = (a - b + c - d) * half
    HH = (a - b - c + d) * half
    return LL, LH, HL, HH


def setup_inputs():
    sc = mx_kscale(K)[::4]
    sk = np.repeat(sc, 4)
    return {"x": bf(np.random.standard_normal((B, C, H, W)) * sc[None, :, None, None]),
            "w_fusion": bf(np.random.standard_normal((O, K, 1, 1)) / np.sqrt(K) / sk[None, :, None, None])}


def reference(x, w_fusion):
    x = f64(x)
    nb, nc_, nh, nw = x.shape
    LL, LH, HL, HH = haar_dwt2(x)
    combined = np.stack([LL, LH, HL, HH], axis=2)
    combined = combined.reshape(nb, nc_ * 4, nh // 2, nw // 2)
    w = f64(w_fusion)[:, :, 0, 0]
    return np.einsum('bchw,oc->bohw', mxq(combined, 1, "e4m3"), mxq(w, 1, "e4m3"), optimize=True)

@@ -1,0 +1,117 @@
+from contextlib import ExitStack
+
+import concourse.mybir as mybir
+from concourse.masks import make_identity
+
+F32 = mybir.dt.float32
+BF16 = mybir.dt.bfloat16
+U32 = mybir.dt.uint32
+U8 = mybir.dt.uint8
+FP8X4 = mybir.dt.float8_e4m3fn_x4
+ADD = mybir.AluOpType.add
+SUBTRACT = mybir.AluOpType.subtract
+
+P = 128
+BANDS = 4
+IMAGES, HEIGHT, WIDTH = 2, 64, 64
+OUT_ROWS, OUT_COLS = HEIGHT // 2, WIDTH // 2
+
+CHUNK_ROWS = 8
+CHUNK_BLOCKS = CHUNK_ROWS * OUT_COLS
+CHUNKS_PER_IMAGE = OUT_ROWS // CHUNK_ROWS
+CHUNKS = IMAGES * CHUNKS_PER_IMAGE
+
+FLOPS = 2 * IMAGES * OUT_ROWS * OUT_COLS * BANDS * P * P
+
+
+def tile_haarwaveletlayer_s_kernel(tc, x, w_fusion, out):
+    nc = tc.nc
+    with ExitStack() as stack:
+        const = stack.enter_context(tc.tile_pool(name="const", bufs=1))
+        image = stack.enter_context(tc.tile_pool(name="image", bufs=CHUNKS))
+        work = stack.enter_context(tc.tile_pool(name="work", bufs=3))
+        psum_w = stack.enter_context(tc.psum_pool(name="psum_w", bufs=1))
+        psum = stack.enter_context(tc.psum_pool(name="psum", bufs=3))
+        stack.enter_context(tc.manual_schedule())
+
+        def load_pixels(g):
+            n, part = divmod(g, CHUNKS_PER_IMAGE)
+            rows = slice(2 * CHUNK_ROWS * part, 2 * CHUNK_ROWS * (part + 1))
+            pixels = image.tile([P, 2 * CHUNK_ROWS * WIDTH], BF16)
+            nc.sync.dma_start(out=pixels[:], in_=x[n, :, rows, :].rearrange("c h w -> c (h w)"))
+            return pixels
+
+        def horizontal(pixels):
+            pairs = pixels[:].rearrange("c (m e) -> c m e", e=2)
+            across = work.tile([P, 2, 2 * CHUNK_BLOCKS], F32)
+            nc.vector.tensor_tensor(out=across[:, 0, :], in0=pairs[:, :, 0], in1=pairs[:, :, 1], op=ADD)
+            nc.vector.tensor_tensor(out=across[:, 1, :], in0=pairs[:, :, 0], in1=pairs[:, :, 1], op=SUBTRACT)
+            return across
+
+        def vertical(across):
+            rows = across[:].rearrange("c s (i r j) -> c s i r j", r=2, j=OUT_COLS)
+            top, bottom = rows[:, :, :, 0, :], rows[:, :, :, 1, :]
+            bands = work.tile([P, BANDS, CHUNK_BLOCKS], F32)
+            planes = bands[:].rearrange("c (s v) (i j) -> c s v i j", v=2, j=OUT_COLS)
+            nc.vector.tensor_tensor(out=planes[:, :, 0, :, :], in0=top, in1=bottom, op=ADD)
+            nc.vector.tensor_tensor(out=planes[:, :, 1, :, :], in0=top, in1=bottom, op=SUBTRACT)
+            return bands
+
+        def group(bands):
+            grouped = work.tile([P, CHUNK_BLOCKS, BANDS], BF16, align_bytes=64)
+            nc.scalar.mul(out=grouped[:], in_=bands[:].rearrange("c t m -> c m t"), mul=0.5)
+            return grouped
+
+        def finish(g, grouped):
+            codes = work.tile([P, CHUNK_BLOCKS], U32, align_bytes=64)
+            scales = work.tile([P, CHUNK_BLOCKS], U8, align_bytes=64)
+            nc.vector.quantize_mx(
+                out=codes[:].bitcast(FP8X4),
+                scales=scales[:],
+                in_=grouped[:].rearrange("c m t -> c (m t)"),
+            )
+            acc = psum.tile([P, CHUNK_BLOCKS], F32)
+            nc.tensor.matmul_mx(
+                out=acc[:],
+                lhsT=w_codes[:].bitcast(FP8X4),
+                lhsT_scale=w_scales[:],
+                rhs=codes[:].bitcast(FP8X4),
+                rhs_scale=scales[:],
+                start=True,
+                stop=True,
+            )
+            result = work.tile([P, CHUNK_BLOCKS], F32)
+            nc.scalar.copy(out=result[:], in_=acc[:])
+            n, part = divmod(g, CHUNKS_PER_IMAGE)
+            rows = slice(CHUNK_ROWS * part, CHUNK_ROWS * (part + 1))
+            nc.sync.dma_start(out=out[n, :, rows, :].rearrange("o i j -> o (i j)"), in_=result[:])
+
+        w_rows = const.tile([P, BANDS * P], BF16)
+        chunk_pixels = [load_pixels(0)]
+        nc.sync.dma_start(out=w_rows[:], in_=w_fusion.rearrange("o k a b -> o (k a b)"))
+        for g in range(1, CHUNKS):
+            chunk_pixels.append(load_pixels(g))
+
+        identity = const.tile([P, P], F32)
+        make_identity(nc, identity[:])
+        w_words = w_rows[:].bitcast(F32).rearrange("o (c u) -> o c u", u=2)
+        w_turned = psum_w.tile([P, 2, P], F32)
+        for u in range(2):
+            nc.tensor.transpose(w_turned[:, u, :], w_words[:, :, u], identity[:])
+        w_grouped = const.tile([P, P * BANDS], BF16, align_bytes=64)
+        nc.scalar.copy(
+            out=w_grouped[:].bitcast(F32).rearrange("c (o u) -> c o u", u=2),
+            in_=w_turned[:].rearrange("c u o -> c o u"),
+        )
+        w_codes = const.tile([P, P], U32, align_bytes=64)
+        w_scales = const.tile([P, P], U8, align_bytes=64)
+
+        chunk_across = {0: horizontal(chunk_pixels[0]), 1: horizontal(chunk_pixels[1])}
+        chunk_grouped = {0: group(vertical(chunk_across[0]))}
+        nc.vector.quantize_mx(out=w_codes[:].bitcast(FP8X4), scales=w_scales[:], in_=w_grouped[:])
+        for g in range(CHUNKS):
+            if g + 2 < CHUNKS:
+                chunk_across[g + 2] = horizontal(chunk_pixels[g + 2])
+            if g + 1 < CHUNKS:
+                chunk_grouped[g + 1] = group(vertical(chunk_across[g + 1]))
+            finish(g, chunk_grouped[g])

@@ -16,7 +16,7 @@ BANDS = 4
 IMAGES, HEIGHT, WIDTH = 2, 64, 64
 OUT_ROWS, OUT_COLS = HEIGHT // 2, WIDTH // 2
 
-CHUNK_ROWS = 8
+CHUNK_ROWS = 4
 CHUNK_BLOCKS = CHUNK_ROWS * OUT_COLS
 CHUNKS_PER_IMAGE = OUT_ROWS // CHUNK_ROWS
 CHUNKS = IMAGES * CHUNKS_PER_IMAGE

@@ -16,102 +16,130 @@ BANDS = 4
 IMAGES, HEIGHT, WIDTH = 2, 64, 64
 OUT_ROWS, OUT_COLS = HEIGHT // 2, WIDTH // 2
 
-CHUNK_ROWS = 4
-CHUNK_BLOCKS = CHUNK_ROWS * OUT_COLS
-CHUNKS_PER_IMAGE = OUT_ROWS // CHUNK_ROWS
-CHUNKS = IMAGES * CHUNKS_PER_IMAGE
+SIZES = ((4, 4, 8, 8, 8), (8, 8, 4, 4, 4, 4))
+assert all(sum(sizes) == OUT_ROWS for sizes in SIZES)
+MAX_BLOCKS = max(max(sizes) for sizes in SIZES) * OUT_COLS
+LAG = 2
 
 FLOPS = 2 * IMAGES * OUT_ROWS * OUT_COLS * BANDS * P * P
 
 
+def chunk_list():
+    chunks = []
+    for n, sizes in enumerate(SIZES):
+        first = 0
+        for rows in sizes:
+            chunks.append((n, first, rows))
+            first += rows
+    return chunks
+
+
 def tile_haarwaveletlayer_s_kernel(tc, x, w_fusion, out):
     nc = tc.nc
+    chunks = chunk_list()
+    count = len(chunks)
     with ExitStack() as stack:
         const = stack.enter_context(tc.tile_pool(name="const", bufs=1))
-        image = stack.enter_context(tc.tile_pool(name="image", bufs=CHUNKS))
-        work = stack.enter_context(tc.tile_pool(name="work", bufs=3))
+        work = stack.enter_context(tc.tile_pool(name="work", bufs=4))
         psum_w = stack.enter_context(tc.psum_pool(name="psum_w", bufs=1))
         psum = stack.enter_context(tc.psum_pool(name="psum", bufs=3))
         stack.enter_context(tc.manual_schedule())
 
         def load_pixels(g):
-            n, part = divmod(g, CHUNKS_PER_IMAGE)
-            rows = slice(2 * CHUNK_ROWS * part, 2 * CHUNK_ROWS * (part + 1))
-            pixels = image.tile([P, 2 * CHUNK_ROWS * WIDTH], BF16)
-            nc.sync.dma_start(out=pixels[:], in_=x[n, :, rows, :].rearrange("c h w -> c (h w)"))
+            n, first, rows = chunks[g]
+            pixels = const.tile([P, 2 * rows * WIDTH], BF16, name="pixels%d" % g)
+            nc.sync.dma_start(
+                out=pixels[:], in_=x[n, :, 2 * first : 2 * (first + rows), :].rearrange("c h w -> c (h w)")
+            )
             return pixels
 
-        def horizontal(pixels):
+        def horizontal(g, pixels):
+            blocks = chunks[g][2] * OUT_COLS
             pairs = pixels[:].rearrange("c (m e) -> c m e", e=2)
-            across = work.tile([P, 2, 2 * CHUNK_BLOCKS], F32)
-            nc.vector.tensor_tensor(out=across[:, 0, :], in0=pairs[:, :, 0], in1=pairs[:, :, 1], op=ADD)
-            nc.vector.tensor_tensor(out=across[:, 1, :], in0=pairs[:, :, 0], in1=pairs[:, :, 1], op=SUBTRACT)
+            across = work.tile([P, 2, 2 * MAX_BLOCKS], F32)
+            nc.vector.tensor_tensor(out=across[:, 0, : 2 * blocks], in0=pairs[:, :, 0], in1=pairs[:, :, 1], op=ADD)
+            nc.vector.tensor_tensor(
+                out=across[:, 1, : 2 * blocks], in0=pairs[:, :, 0], in1=pairs[:, :, 1], op=SUBTRACT
+            )
             return across
 
-        def vertical(across):
-            rows = across[:].rearrange("c s (i r j) -> c s i r j", r=2, j=OUT_COLS)
+        def vertical(g, across):
+            blocks = chunks[g][2] * OUT_COLS
+            rows = across[:, :, : 2 * blocks].rearrange("c s (i r j) -> c s i r j", r=2, j=OUT_COLS)
             top, bottom = rows[:, :, :, 0, :], rows[:, :, :, 1, :]
-            bands = work.tile([P, BANDS, CHUNK_BLOCKS], F32)
-            planes = bands[:].rearrange("c (s v) (i j) -> c s v i j", v=2, j=OUT_COLS)
+            bands = work.tile([P, BANDS, MAX_BLOCKS], F32)
+            planes = bands[:, :, :blocks].rearrange("c (s v) (i j) -> c s v i j", v=2, j=OUT_COLS)
             nc.vector.tensor_tensor(out=planes[:, :, 0, :, :], in0=top, in1=bottom, op=ADD)
             nc.vector.tensor_tensor(out=planes[:, :, 1, :, :], in0=top, in1=bottom, op=SUBTRACT)
             return bands
 
-        def group(bands):
-            grouped = work.tile([P, CHUNK_BLOCKS, BANDS], BF16, align_bytes=64)
-            nc.scalar.mul(out=grouped[:], in_=bands[:].rearrange("c t m -> c m t"), mul=0.5)
+        def group(g, bands):
+            blocks = chunks[g][2] * OUT_COLS
+            grouped = work.tile([P, MAX_BLOCKS * BANDS], BF16, align_bytes=64)
+            nc.scalar.mul(
+                out=grouped[:, : blocks * BANDS].rearrange("c (m t) -> c m t", t=BANDS),
+                in_=bands[:, :, :blocks].rearrange("c t m -> c m t"),
+                mul=0.5,
+            )
             return grouped
 
         def finish(g, grouped):
-            codes = work.tile([P, CHUNK_BLOCKS], U32, align_bytes=64)
-            scales = work.tile([P, CHUNK_BLOCKS], U8, align_bytes=64)
+            n, first, rows = chunks[g]
+            blocks = rows * OUT_COLS
+            codes = work.tile([P, MAX_BLOCKS], U32, align_bytes=64)
+            scales = work.tile([P, MAX_BLOCKS], U8, align_bytes=64)
             nc.vector.quantize_mx(
-                out=codes[:].bitcast(FP8X4),
-                scales=scales[:],
-                in_=grouped[:].rearrange("c m t -> c (m t)"),
+                out=codes[:, :blocks].bitcast(FP8X4), scales=scales[:, :blocks], in_=grouped[:, : blocks * BANDS]
             )
-            acc = psum.tile([P, CHUNK_BLOCKS], F32)
+            acc = psum.tile([P, MAX_BLOCKS], F32)
             nc.tensor.matmul_mx(
-                out=acc[:],
+                out=acc[:, :blocks],
                 lhsT=w_codes[:].bitcast(FP8X4),
                 lhsT_scale=w_scales[:],
-                rhs=codes[:].bitcast(FP8X4),
-                rhs_scale=scales[:],
+                rhs=codes[:, :blocks].bitcast(FP8X4),
+                rhs_scale=scales[:, :blocks],
                 start=True,
                 stop=True,
             )
-            result = work.tile([P, CHUNK_BLOCKS], F32)
-            nc.scalar.copy(out=result[:], in_=acc[:])
-            n, part = divmod(g, CHUNKS_PER_IMAGE)
-            rows = slice(CHUNK_ROWS * part, CHUNK_ROWS * (part + 1))
-            nc.sync.dma_start(out=out[n, :, rows, :].rearrange("o i j -> o (i j)"), in_=result[:])
+            result = work.tile([P, MAX_BLOCKS], F32)
+            nc.scalar.copy(out=result[:, :blocks], in_=acc[:, :blocks])
+            nc.sync.dma_start(
+                out=out[n, :, first : first + rows, :].rearrange("o i j -> o (i j)"), in_=result[:, :blocks]
+            )
 
         w_rows = const.tile([P, BANDS * P], BF16)
-        chunk_pixels = [load_pixels(0)]
-        nc.sync.dma_start(out=w_rows[:], in_=w_fusion.rearrange("o k a b -> o (k a b)"))
-        for g in range(1, CHUNKS):
+        chunk_pixels = []
+        for g in range(count):
+            if g == 1:
+                nc.sync.dma_start(out=w_rows[:], in_=w_fusion.rearrange("o k a b -> o (k a b)"))
             chunk_pixels.append(load_pixels(g))
 
         identity = const.tile([P, P], F32)
         make_identity(nc, identity[:])
-        w_words = w_rows[:].bitcast(F32).rearrange("o (c u) -> o c u", u=2)
-        w_turned = psum_w.tile([P, 2, P], F32)
-        for u in range(2):
-            nc.tensor.transpose(w_turned[:, u, :], w_words[:, :, u], identity[:])
         w_grouped = const.tile([P, P * BANDS], BF16, align_bytes=64)
-        nc.scalar.copy(
-            out=w_grouped[:].bitcast(F32).rearrange("c (o u) -> c o u", u=2),
-            in_=w_turned[:].rearrange("c u o -> c o u"),
-        )
         w_codes = const.tile([P, P], U32, align_bytes=64)
         w_scales = const.tile([P, P], U8, align_bytes=64)
 
-        chunk_across = {0: horizontal(chunk_pixels[0]), 1: horizontal(chunk_pixels[1])}
-        chunk_grouped = {0: group(vertical(chunk_across[0]))}
-        nc.vector.quantize_mx(out=w_codes[:].bitcast(FP8X4), scales=w_scales[:], in_=w_grouped[:])
-        for g in range(CHUNKS):
-            if g + 2 < CHUNKS:
-                chunk_across[g + 2] = horizontal(chunk_pixels[g + 2])
-            if g + 1 < CHUNKS:
-                chunk_grouped[g + 1] = group(vertical(chunk_across[g + 1]))
-            finish(g, chunk_grouped[g])
+        def turn_weights():
+            w_words = w_rows[:].bitcast(F32).rearrange("o (c u) -> o c u", u=2)
+            w_turned = psum_w.tile([P, 2, P], F32)
+            for u in range(2):
+                nc.tensor.transpose(w_turned[:, u, :], w_words[:, :, u], identity[:])
+            nc.scalar.copy(
+                out=w_grouped[:].bitcast(F32).rearrange("c (o u) -> c o u", u=2),
+                in_=w_turned[:].rearrange("c u o -> c o u"),
+            )
+
+        chunk_across = {}
+        chunk_grouped = {}
+        for g in range(-LAG - 1, count):
+            if 0 <= g + LAG + 1 < count:
+                chunk_across[g + LAG + 1] = horizontal(g + LAG + 1, chunk_pixels[g + LAG + 1])
+            if 0 <= g + LAG < count:
+                chunk_grouped[g + LAG] = group(g + LAG, vertical(g + LAG, chunk_across[g + LAG]))
+            if g == -3:
+                turn_weights()
+            if g == 0:
+                nc.vector.quantize_mx(out=w_codes[:].bitcast(FP8X4), scales=w_scales[:], in_=w_grouped[:])
+            if g >= 0:
+                finish(g, chunk_grouped[g])

@@ -83,6 +83,16 @@ def tile_haarwaveletlayer_s_kernel(tc, x, w_fusion, out):
             )
             return grouped
 
+        def group_on_vector(g, bands):
+            blocks = chunks[g][2] * OUT_COLS
+            grouped = work.tile([P, MAX_BLOCKS * BANDS], BF16, align_bytes=64)
+            nc.vector.tensor_scalar_mul(
+                out=grouped[:, : blocks * BANDS].rearrange("c (m t) -> c m t", t=BANDS),
+                in0=bands[:, :, :blocks].rearrange("c t m -> c m t"),
+                scalar1=0.5,
+            )
+            return grouped
+
         def finish(g, grouped):
             n, first, rows = chunks[g]
             blocks = rows * OUT_COLS
@@ -136,10 +146,14 @@ def tile_haarwaveletlayer_s_kernel(tc, x, w_fusion, out):
             if 0 <= g + LAG + 1 < count:
                 chunk_across[g + LAG + 1] = horizontal(g + LAG + 1, chunk_pixels[g + LAG + 1])
             if 0 <= g + LAG < count:
-                chunk_grouped[g + LAG] = group(g + LAG, vertical(g + LAG, chunk_across[g + LAG]))
+                bands = vertical(g + LAG, chunk_across[g + LAG])
+                if g + LAG < count - 1:
+                    chunk_grouped[g + LAG] = group(g + LAG, bands)
             if g == -3:
                 turn_weights()
             if g == 0:
                 nc.vector.quantize_mx(out=w_codes[:].bitcast(FP8X4), scales=w_scales[:], in_=w_grouped[:])
             if g >= 0:
                 finish(g, chunk_grouped[g])
+            if g + LAG == count - 1:
+                chunk_grouped[count - 1] = group_on_vector(count - 1, bands)

@@ -20,6 +20,7 @@ SIZES = ((4, 4, 8, 8, 8), (8, 8, 4, 4, 4, 4))
 assert all(sum(sizes) == OUT_ROWS for sizes in SIZES)
 MAX_BLOCKS = max(max(sizes) for sizes in SIZES) * OUT_COLS
 LAG = 2
+MAX_TOP = 4 * OUT_COLS
 
 FLOPS = 2 * IMAGES * OUT_ROWS * OUT_COLS * BANDS * P * P
 
@@ -41,8 +42,10 @@ def tile_haarwaveletlayer_s_kernel(tc, x, w_fusion, out):
     with ExitStack() as stack:
         const = stack.enter_context(tc.tile_pool(name="const", bufs=1))
         work = stack.enter_context(tc.tile_pool(name="work", bufs=4))
+        results = stack.enter_context(tc.tile_pool(name="results", bufs=count))
         psum_w = stack.enter_context(tc.psum_pool(name="psum_w", bufs=1))
         psum = stack.enter_context(tc.psum_pool(name="psum", bufs=3))
+        psum_t = stack.enter_context(tc.psum_pool(name="psum_t", bufs=1))
         stack.enter_context(tc.manual_schedule())
 
         def load_pixels(g):
@@ -52,6 +55,37 @@ def tile_haarwaveletlayer_s_kernel(tc, x, w_fusion, out):
                 out=pixels[:], in_=x[n, :, 2 * first : 2 * (first + rows), :].rearrange("c h w -> c (h w)")
             )
             return pixels
+
+        def top_rows_on_tensor(g, pixels):
+            picked = pixels[:].rearrange("c (i r j e) -> c r e i j", r=2, j=OUT_COLS, e=2)
+            left, right = picked[:, 0, 0, :, :], picked[:, 0, 1, :, :]
+            top = psum_t.tile([P, 2, MAX_TOP], F32)
+            for s, second in enumerate((plus_one, minus_one)):
+                target = top[:, s, : chunks[g][2] * OUT_COLS].rearrange("c (i j) -> c i j", j=OUT_COLS)
+                nc.tensor.matmul(out=target, lhsT=plus_one[:], rhs=left, start=True, stop=False)
+                nc.tensor.matmul(out=target, lhsT=second[:], rhs=right, start=False, stop=True)
+            return top
+
+        def horizontal_bottom(g, pixels):
+            blocks = chunks[g][2] * OUT_COLS
+            picked = pixels[:].rearrange("c (i r j e) -> c r e i j", r=2, j=OUT_COLS, e=2)
+            left, right = picked[:, 1, 0, :, :], picked[:, 1, 1, :, :]
+            across = work.tile([P, 2, 2 * MAX_BLOCKS], F32)
+            for s, op in enumerate((ADD, SUBTRACT)):
+                nc.vector.tensor_tensor(
+                    out=across[:, s, :blocks].rearrange("c (i j) -> c i j", j=OUT_COLS), in0=left, in1=right, op=op
+                )
+            return across
+
+        def vertical_mixed(g, top, across):
+            blocks = chunks[g][2] * OUT_COLS
+            bands = work.tile([P, BANDS, MAX_BLOCKS], F32)
+            planes = bands[:, :, :blocks].rearrange("c (s v) m -> c s v m", v=2)
+            nc.vector.tensor_tensor(out=planes[:, :, 0, :], in0=top[:, :, :blocks], in1=across[:, :, :blocks], op=ADD)
+            nc.vector.tensor_tensor(
+                out=planes[:, :, 1, :], in0=top[:, :, :blocks], in1=across[:, :, :blocks], op=SUBTRACT
+            )
+            return bands
 
         def horizontal(g, pixels):
             blocks = chunks[g][2] * OUT_COLS
@@ -111,7 +145,7 @@ def tile_haarwaveletlayer_s_kernel(tc, x, w_fusion, out):
                 start=True,
                 stop=True,
             )
-            result = work.tile([P, MAX_BLOCKS], F32)
+            result = results.tile([P, MAX_BLOCKS], F32)
             nc.scalar.copy(out=result[:, :blocks], in_=acc[:, :blocks])
             nc.sync.dma_start(
                 out=out[n, :, first : first + rows, :].rearrange("o i j -> o (i j)"), in_=result[:, :blocks]
@@ -126,6 +160,10 @@ def tile_haarwaveletlayer_s_kernel(tc, x, w_fusion, out):
 
         identity = const.tile([P, P], F32)
         make_identity(nc, identity[:])
+        plus_one = const.tile([P, P], BF16)
+        make_identity(nc, plus_one[:])
+        minus_one = const.tile([P, P], BF16)
+        nc.scalar.mul(out=minus_one[:], in_=plus_one[:], mul=-1.0)
         w_grouped = const.tile([P, P * BANDS], BF16, align_bytes=64)
         w_codes = const.tile([P, P], U32, align_bytes=64)
         w_scales = const.tile([P, P], U8, align_bytes=64)
@@ -144,13 +182,21 @@ def tile_haarwaveletlayer_s_kernel(tc, x, w_fusion, out):
         chunk_grouped = {}
         for g in range(-LAG - 1, count):
             if 0 <= g + LAG + 1 < count:
-                chunk_across[g + LAG + 1] = horizontal(g + LAG + 1, chunk_pixels[g + LAG + 1])
+                if g + LAG + 1 == count - 1:
+                    chunk_across[count - 1] = horizontal_bottom(count - 1, chunk_pixels[count - 1])
+                else:
+                    chunk_across[g + LAG + 1] = horizontal(g + LAG + 1, chunk_pixels[g + LAG + 1])
             if 0 <= g + LAG < count:
-                bands = vertical(g + LAG, chunk_across[g + LAG])
+                if g + LAG == count - 1:
+                    bands = vertical_mixed(count - 1, last_top, chunk_across[count - 1])
+                else:
+                    bands = vertical(g + LAG, chunk_across[g + LAG])
                 if g + LAG < count - 1:
                     chunk_grouped[g + LAG] = group(g + LAG, bands)
             if g == -3:
                 turn_weights()
+            if g == 1:
+                last_top = top_rows_on_tensor(count - 1, chunk_pixels[count - 1])
             if g == 0:
                 nc.vector.quantize_mx(out=w_codes[:].bitcast(FP8X4), scales=w_scales[:], in_=w_grouped[:])
             if g >= 0:

@@ -154,7 +154,7 @@ def tile_haarwaveletlayer_s_kernel(tc, x, w_fusion, out):
         w_rows = const.tile([P, BANDS * P], BF16)
         chunk_pixels = []
         for g in range(count):
-            if g == 1:
+            if g == 3:
                 nc.sync.dma_start(out=w_rows[:], in_=w_fusion.rearrange("o k a b -> o (k a b)"))
             chunk_pixels.append(load_pixels(g))
 
@@ -193,7 +193,7 @@ def tile_haarwaveletlayer_s_kernel(tc, x, w_fusion, out):
                     bands = vertical(g + LAG, chunk_across[g + LAG])
                 if g + LAG < count - 1:
                     chunk_grouped[g + LAG] = group(g + LAG, bands)
-            if g == -3:
+            if g == -1:
                 turn_weights()
             if g == 1:
                 last_top = top_rows_on_tensor(count - 1, chunk_pixels[count - 1])

@@ -56,6 +56,24 @@ def tile_haarwaveletlayer_s_kernel(tc, x, w_fusion, out):
             )
             return pixels
 
+        def load_first_half(half):
+            rows = chunks[0][2] // 2
+            pixels = const.tile([P, 2 * rows * WIDTH], BF16, name="first%d" % half)
+            nc.sync.dma_start(
+                out=pixels[:], in_=x[0, :, 2 * rows * half : 2 * rows * (half + 1), :].rearrange("c h w -> c (h w)")
+            )
+            return pixels
+
+        def horizontal_first(halves):
+            blocks = chunks[0][2] * OUT_COLS
+            across = work.tile([P, 2, 2 * MAX_BLOCKS], F32)
+            for half, pixels in enumerate(halves):
+                pairs = pixels[:].rearrange("c (m e) -> c m e", e=2)
+                span = slice(blocks * half, blocks * (half + 1))
+                nc.vector.tensor_tensor(out=across[:, 0, span], in0=pairs[:, :, 0], in1=pairs[:, :, 1], op=ADD)
+                nc.vector.tensor_tensor(out=across[:, 1, span], in0=pairs[:, :, 0], in1=pairs[:, :, 1], op=SUBTRACT)
+            return across
+
         def top_rows_on_tensor(g, pixels):
             picked = pixels[:].rearrange("c (i r j e) -> c r e i j", r=2, j=OUT_COLS, e=2)
             left, right = picked[:, 0, 0, :, :], picked[:, 0, 1, :, :]
@@ -156,7 +174,10 @@ def tile_haarwaveletlayer_s_kernel(tc, x, w_fusion, out):
         for g in range(count):
             if g == 3:
                 nc.sync.dma_start(out=w_rows[:], in_=w_fusion.rearrange("o k a b -> o (k a b)"))
-            chunk_pixels.append(load_pixels(g))
+            if g == 0:
+                chunk_pixels.append([load_first_half(0), load_first_half(1)])
+            else:
+                chunk_pixels.append(load_pixels(g))
 
         identity = const.tile([P, P], F32)
         make_identity(nc, identity[:])
@@ -184,6 +205,8 @@ def tile_haarwaveletlayer_s_kernel(tc, x, w_fusion, out):
             if 0 <= g + LAG + 1 < count:
                 if g + LAG + 1 == count - 1:
                     chunk_across[count - 1] = horizontal_bottom(count - 1, chunk_pixels[count - 1])
+                elif g + LAG + 1 == 0:
+                    chunk_across[0] = horizontal_first(chunk_pixels[0])
                 else:
                     chunk_across[g + LAG + 1] = horizontal(g + LAG + 1, chunk_pixels[g + LAG + 1])
             if 0 <= g + LAG < count:

@@ -20,7 +20,8 @@ SIZES = ((4, 4, 8, 8, 8), (8, 8, 4, 4, 4, 4))
 assert all(sum(sizes) == OUT_ROWS for sizes in SIZES)
 MAX_BLOCKS = max(max(sizes) for sizes in SIZES) * OUT_COLS
 LAG = 2
-MAX_TOP = 4 * OUT_COLS
+ROW_PIXELS = 2 * WIDTH
+MIXED_ROWS = 2
 
 FLOPS = 2 * IMAGES * OUT_ROWS * OUT_COLS * BANDS * P * P
 
@@ -46,6 +47,7 @@ def tile_haarwaveletlayer_s_kernel(tc, x, w_fusion, out):
         psum_w = stack.enter_context(tc.psum_pool(name="psum_w", bufs=1))
         psum = stack.enter_context(tc.psum_pool(name="psum", bufs=3))
         psum_t = stack.enter_context(tc.psum_pool(name="psum_t", bufs=1))
+        psum_h = stack.enter_context(tc.psum_pool(name="psum_h", bufs=2))
         stack.enter_context(tc.manual_schedule())
 
         def load_pixels(g):
@@ -64,6 +66,9 @@ def tile_haarwaveletlayer_s_kernel(tc, x, w_fusion, out):
             )
             return pixels
 
+        def vector_rows(g):
+            return chunks[g][2] - (MIXED_ROWS if g == count - 2 else 0)
+
         def horizontal_first(halves):
             blocks = chunks[0][2] * OUT_COLS
             across = work.tile([P, 2, 2 * MAX_BLOCKS], F32)
@@ -74,40 +79,9 @@ def tile_haarwaveletlayer_s_kernel(tc, x, w_fusion, out):
                 nc.vector.tensor_tensor(out=across[:, 1, span], in0=pairs[:, :, 0], in1=pairs[:, :, 1], op=SUBTRACT)
             return across
 
-        def top_rows_on_tensor(g, pixels):
-            picked = pixels[:].rearrange("c (i r j e) -> c r e i j", r=2, j=OUT_COLS, e=2)
-            left, right = picked[:, 0, 0, :, :], picked[:, 0, 1, :, :]
-            top = psum_t.tile([P, 2, MAX_TOP], F32)
-            for s, second in enumerate((plus_one, minus_one)):
-                target = top[:, s, : chunks[g][2] * OUT_COLS].rearrange("c (i j) -> c i j", j=OUT_COLS)
-                nc.tensor.matmul(out=target, lhsT=plus_one[:], rhs=left, start=True, stop=False)
-                nc.tensor.matmul(out=target, lhsT=second[:], rhs=right, start=False, stop=True)
-            return top
-
-        def horizontal_bottom(g, pixels):
-            blocks = chunks[g][2] * OUT_COLS
-            picked = pixels[:].rearrange("c (i r j e) -> c r e i j", r=2, j=OUT_COLS, e=2)
-            left, right = picked[:, 1, 0, :, :], picked[:, 1, 1, :, :]
-            across = work.tile([P, 2, 2 * MAX_BLOCKS], F32)
-            for s, op in enumerate((ADD, SUBTRACT)):
-                nc.vector.tensor_tensor(
-                    out=across[:, s, :blocks].rearrange("c (i j) -> c i j", j=OUT_COLS), in0=left, in1=right, op=op
-                )
-            return across
-
-        def vertical_mixed(g, top, across):
-            blocks = chunks[g][2] * OUT_COLS
-            bands = work.tile([P, BANDS, MAX_BLOCKS], F32)
-            planes = bands[:, :, :blocks].rearrange("c (s v) m -> c s v m", v=2)
-            nc.vector.tensor_tensor(out=planes[:, :, 0, :], in0=top[:, :, :blocks], in1=across[:, :, :blocks], op=ADD)
-            nc.vector.tensor_tensor(
-                out=planes[:, :, 1, :], in0=top[:, :, :blocks], in1=across[:, :, :blocks], op=SUBTRACT
-            )
-            return bands
-
         def horizontal(g, pixels):
-            blocks = chunks[g][2] * OUT_COLS
-            pairs = pixels[:].rearrange("c (m e) -> c m e", e=2)
+            blocks = vector_rows(g) * OUT_COLS
+            pairs = pixels[:, : 4 * blocks].rearrange("c (m e) -> c m e", e=2)
             across = work.tile([P, 2, 2 * MAX_BLOCKS], F32)
             nc.vector.tensor_tensor(out=across[:, 0, : 2 * blocks], in0=pairs[:, :, 0], in1=pairs[:, :, 1], op=ADD)
             nc.vector.tensor_tensor(
@@ -116,7 +90,7 @@ def tile_haarwaveletlayer_s_kernel(tc, x, w_fusion, out):
             return across
 
         def vertical(g, across):
-            blocks = chunks[g][2] * OUT_COLS
+            blocks = vector_rows(g) * OUT_COLS
             rows = across[:, :, : 2 * blocks].rearrange("c s (i r j) -> c s i r j", r=2, j=OUT_COLS)
             top, bottom = rows[:, :, :, 0, :], rows[:, :, :, 1, :]
             bands = work.tile([P, BANDS, MAX_BLOCKS], F32)
@@ -135,15 +109,38 @@ def tile_haarwaveletlayer_s_kernel(tc, x, w_fusion, out):
             )
             return grouped
 
-        def group_on_vector(g, bands):
-            blocks = chunks[g][2] * OUT_COLS
-            grouped = work.tile([P, MAX_BLOCKS * BANDS], BF16, align_bytes=64)
+        def group_on_vector(g, bands, grouped):
+            blocks = vector_rows(g) * OUT_COLS
             nc.vector.tensor_scalar_mul(
                 out=grouped[:, : blocks * BANDS].rearrange("c (m t) -> c m t", t=BANDS),
                 in0=bands[:, :, :blocks].rearrange("c t m -> c m t"),
                 scalar1=0.5,
             )
-            return grouped
+
+        def turn_pixels(parts):
+            total = sum(rows for pixels, first, rows in parts)
+            turned = psum_t.tile([P, total, P], BF16)
+            u = 0
+            for pixels, first, rows in parts:
+                for i in range(first, first + rows):
+                    nc.tensor.transpose(turned[:, u, :], pixels[:, ROW_PIXELS * i : ROW_PIXELS * (i + 1)], plus_one[:])
+                    u += 1
+            turned_pixels = const.tile([P, total, P], BF16)
+            nc.scalar.copy(out=turned_pixels[:], in_=turned[:])
+            return turned_pixels
+
+        def haar_rows(turned_pixels, first, rows):
+            made = psum_h.tile([P, 4, P], F32)
+            for i in range(rows):
+                nc.tensor.matmul(
+                    out=made[:, i, :], lhsT=turned_pixels[:, first + i, :], rhs=haar[:], start=True, stop=True
+                )
+            return made
+
+        def round_rows(made, rows, target):
+            nc.scalar.mul(
+                out=target.rearrange("c (i m) -> c i m", m=P), in_=made[:, :rows, :], mul=0.5
+            )
 
         def finish(g, grouped):
             n, first, rows = chunks[g]
@@ -179,12 +176,19 @@ def tile_haarwaveletlayer_s_kernel(tc, x, w_fusion, out):
             else:
                 chunk_pixels.append(load_pixels(g))
 
-        identity = const.tile([P, P], F32)
-        make_identity(nc, identity[:])
         plus_one = const.tile([P, P], BF16)
         make_identity(nc, plus_one[:])
-        minus_one = const.tile([P, P], BF16)
-        nc.scalar.mul(out=minus_one[:], in_=plus_one[:], mul=-1.0)
+        identity = const.tile([P, P], F32)
+        nc.scalar.copy(out=identity[:], in_=plus_one[:])
+        haar = const.tile([P, P], BF16)
+        sums = const.tile([P, 2, P // 2], BF16)
+        pixel_pairs = plus_one[:].rearrange("q (m e) -> q m e", e=2)
+        for s, op in enumerate((ADD, SUBTRACT)):
+            nc.vector.tensor_tensor(out=sums[:, s, :], in0=pixel_pairs[:, :, 0], in1=pixel_pairs[:, :, 1], op=op)
+        row_pairs = sums[:].rearrange("q s (r j) -> q s r j", r=2)
+        bands_of = haar[:].rearrange("q (j s v) -> q s v j", s=2, v=2)
+        for v, op in enumerate((ADD, SUBTRACT)):
+            nc.vector.tensor_tensor(out=bands_of[:, :, v, :], in0=row_pairs[:, :, 0, :], in1=row_pairs[:, :, 1, :], op=op)
         w_grouped = const.tile([P, P * BANDS], BF16, align_bytes=64)
         w_codes = const.tile([P, P], U32, align_bytes=64)
         w_scales = const.tile([P, P], U8, align_bytes=64)
@@ -199,30 +203,37 @@ def tile_haarwaveletlayer_s_kernel(tc, x, w_fusion, out):
                 in_=w_turned[:].rearrange("c u o -> c o u"),
             )
 
+        last = count - 2
         chunk_across = {}
         chunk_grouped = {}
-        for g in range(-LAG - 1, count):
-            if 0 <= g + LAG + 1 < count:
-                if g + LAG + 1 == count - 1:
-                    chunk_across[count - 1] = horizontal_bottom(count - 1, chunk_pixels[count - 1])
-                elif g + LAG + 1 == 0:
+        for g in range(-LAG - 1, last + 1):
+            if g + LAG + 1 <= last:
+                if g + LAG + 1 == 0:
                     chunk_across[0] = horizontal_first(chunk_pixels[0])
                 else:
                     chunk_across[g + LAG + 1] = horizontal(g + LAG + 1, chunk_pixels[g + LAG + 1])
-            if 0 <= g + LAG < count:
-                if g + LAG == count - 1:
-                    bands = vertical_mixed(count - 1, last_top, chunk_across[count - 1])
-                else:
-                    bands = vertical(g + LAG, chunk_across[g + LAG])
-                if g + LAG < count - 1:
+            if 0 <= g + LAG <= last:
+                bands = vertical(g + LAG, chunk_across[g + LAG])
+                if g + LAG < last:
                     chunk_grouped[g + LAG] = group(g + LAG, bands)
             if g == -1:
                 turn_weights()
-            if g == 1:
-                last_top = top_rows_on_tensor(count - 1, chunk_pixels[count - 1])
             if g == 0:
                 nc.vector.quantize_mx(out=w_codes[:].bitcast(FP8X4), scales=w_scales[:], in_=w_grouped[:])
             if g >= 0:
                 finish(g, chunk_grouped[g])
-            if g + LAG == count - 1:
-                chunk_grouped[count - 1] = group_on_vector(count - 1, bands)
+            if g == 1:
+                turned_pixels = turn_pixels(((chunk_pixels[last], MIXED_ROWS, MIXED_ROWS), (chunk_pixels[last + 1], 0, 4)))
+            if g == 2:
+                made_mixed = haar_rows(turned_pixels, 0, MIXED_ROWS)
+                made_last = haar_rows(turned_pixels, MIXED_ROWS, 4)
+            if g == 3:
+                half = MIXED_ROWS * OUT_COLS * BANDS
+                for c in (last, last + 1):
+                    chunk_grouped[c] = const.tile([P, 4 * OUT_COLS * BANDS], BF16, align_bytes=64, name="grouped%d" % c)
+                round_rows(made_mixed, MIXED_ROWS, chunk_grouped[last][:, half : 2 * half])
+                round_rows(made_last, 4, chunk_grouped[last + 1][:])
+            if g == 5:
+                finish(last + 1, chunk_grouped[last + 1])
+            if g + LAG == last:
+                group_on_vector(last, bands, chunk_grouped[last])

@@ -125,7 +125,10 @@ def tile_haarwaveletlayer_s_kernel(tc, x, w_fusion, out):
                 for i in range(first, first + rows):
                     nc.tensor.transpose(turned[:, u, :], pixels[:, ROW_PIXELS * i : ROW_PIXELS * (i + 1)], plus_one[:])
                     u += 1
-            turned_pixels = const.tile([P, total, P], BF16)
+            return turned
+
+        def copy_turned(turned):
+            turned_pixels = const.tile([P, MIXED_ROWS + 4, P], BF16)
             nc.scalar.copy(out=turned_pixels[:], in_=turned[:])
             return turned_pixels
 
@@ -222,17 +225,20 @@ def tile_haarwaveletlayer_s_kernel(tc, x, w_fusion, out):
                 nc.vector.quantize_mx(out=w_codes[:].bitcast(FP8X4), scales=w_scales[:], in_=w_grouped[:])
             if g >= 0:
                 finish(g, chunk_grouped[g])
+            if g == 0:
+                turned = turn_pixels(((chunk_pixels[last], MIXED_ROWS, MIXED_ROWS), (chunk_pixels[last + 1], 0, 4)))
             if g == 1:
-                turned_pixels = turn_pixels(((chunk_pixels[last], MIXED_ROWS, MIXED_ROWS), (chunk_pixels[last + 1], 0, 4)))
+                turned_pixels = copy_turned(turned)
             if g == 2:
                 made_mixed = haar_rows(turned_pixels, 0, MIXED_ROWS)
                 made_last = haar_rows(turned_pixels, MIXED_ROWS, 4)
-            if g == 3:
                 half = MIXED_ROWS * OUT_COLS * BANDS
                 for c in (last, last + 1):
                     chunk_grouped[c] = const.tile([P, 4 * OUT_COLS * BANDS], BF16, align_bytes=64, name="grouped%d" % c)
-                round_rows(made_mixed, MIXED_ROWS, chunk_grouped[last][:, half : 2 * half])
+            if g == 3:
                 round_rows(made_last, 4, chunk_grouped[last + 1][:])
+            if g == 4:
+                round_rows(made_mixed, MIXED_ROWS, chunk_grouped[last][:, half : 2 * half])
             if g == 5:
                 finish(last + 1, chunk_grouped[last + 1])
             if g + LAG == last:

@@ -103,8 +103,8 @@ def tile_haarwaveletlayer_s_kernel(tc, x, w_fusion, out):
             blocks = chunks[g][2] * OUT_COLS
             grouped = work.tile([P, MAX_BLOCKS * BANDS], BF16, align_bytes=64)
             nc.scalar.mul(
-                out=grouped[:, : blocks * BANDS].rearrange("c (m t) -> c m t", t=BANDS),
-                in_=bands[:, :, :blocks].rearrange("c t m -> c m t"),
+                out=grouped[:, : blocks * BANDS].rearrange("c (m i t) -> c m t i", t=BANDS, i=4),
+                in_=bands[:, :, :blocks].rearrange("c t (m i) -> c m t i", i=4),
                 mul=0.5,
             )
             return grouped

from contextlib import ExitStack

import concourse.mybir as mybir
from concourse.masks import make_identity

F32 = mybir.dt.float32
BF16 = mybir.dt.bfloat16
U32 = mybir.dt.uint32
U8 = mybir.dt.uint8
FP8X4 = mybir.dt.float8_e4m3fn_x4
ADD = mybir.AluOpType.add
SUBTRACT = mybir.AluOpType.subtract

P = 128
BANDS = 4
IMAGES, HEIGHT, WIDTH = 2, 64, 64
OUT_ROWS, OUT_COLS = HEIGHT // 2, WIDTH // 2

SIZES = ((4, 4, 8, 8, 8), (8, 8, 4, 4, 4, 4))
assert all(sum(sizes) == OUT_ROWS for sizes in SIZES)
MAX_BLOCKS = max(max(sizes) for sizes in SIZES) * OUT_COLS
LAG = 2
ROW_PIXELS = 2 * WIDTH
MIXED_ROWS = 2

FLOPS = 2 * IMAGES * OUT_ROWS * OUT_COLS * BANDS * P * P


def chunk_list():
    chunks = []
    for n, sizes in enumerate(SIZES):
        first = 0
        for rows in sizes:
            chunks.append((n, first, rows))
            first += rows
    return chunks


def tile_haarwaveletlayer_s_kernel(tc, x, w_fusion, out):
    nc = tc.nc
    chunks = chunk_list()
    count = len(chunks)
    with ExitStack() as stack:
        const = stack.enter_context(tc.tile_pool(name="const", bufs=1))
        work = stack.enter_context(tc.tile_pool(name="work", bufs=4))
        results = stack.enter_context(tc.tile_pool(name="results", bufs=count))
        psum_w = stack.enter_context(tc.psum_pool(name="psum_w", bufs=1))
        psum = stack.enter_context(tc.psum_pool(name="psum", bufs=3))
        psum_t = stack.enter_context(tc.psum_pool(name="psum_t", bufs=1))
        psum_h = stack.enter_context(tc.psum_pool(name="psum_h", bufs=2))
        stack.enter_context(tc.manual_schedule())

        def load_pixels(g):
            n, first, rows = chunks[g]
            pixels = const.tile([P, 2 * rows * WIDTH], BF16, name="pixels%d" % g)
            nc.sync.dma_start(
                out=pixels[:], in_=x[n, :, 2 * first : 2 * (first + rows), :].rearrange("c h w -> c (h w)")
            )
            return pixels

        def load_first_half(half):
            rows = chunks[0][2] // 2
            pixels = const.tile([P, 2 * rows * WIDTH], BF16, name="first%d" % half)
            nc.sync.dma_start(
                out=pixels[:], in_=x[0, :, 2 * rows * half : 2 * rows * (half + 1), :].rearrange("c h w -> c (h w)")
            )
            return pixels

        def vector_rows(g):
            return chunks[g][2] - (MIXED_ROWS if g == count - 2 else 0)

        def horizontal_first(halves):
            blocks = chunks[0][2] * OUT_COLS
            across = work.tile([P, 2, 2 * MAX_BLOCKS], F32)
            for half, pixels in enumerate(halves):
                pairs = pixels[:].rearrange("c (m e) -> c m e", e=2)
                span = slice(blocks * half, blocks * (half + 1))
                nc.vector.tensor_tensor(out=across[:, 0, span], in0=pairs[:, :, 0], in1=pairs[:, :, 1], op=ADD)
                nc.vector.tensor_tensor(out=across[:, 1, span], in0=pairs[:, :, 0], in1=pairs[:, :, 1], op=SUBTRACT)
            return across

        def horizontal(g, pixels):
            blocks = vector_rows(g) * OUT_COLS
            pairs = pixels[:, : 4 * blocks].rearrange("c (m e) -> c m e", e=2)
            across = work.tile([P, 2, 2 * MAX_BLOCKS], F32)
            nc.vector.tensor_tensor(out=across[:, 0, : 2 * blocks], in0=pairs[:, :, 0], in1=pairs[:, :, 1], op=ADD)
            nc.vector.tensor_tensor(
                out=across[:, 1, : 2 * blocks], in0=pairs[:, :, 0], in1=pairs[:, :, 1], op=SUBTRACT
            )
            return across

        def vertical(g, across):
            blocks = vector_rows(g) * OUT_COLS
            rows = across[:, :, : 2 * blocks].rearrange("c s (i r j) -> c s i r j", r=2, j=OUT_COLS)
            top, bottom = rows[:, :, :, 0, :], rows[:, :, :, 1, :]
            bands = work.tile([P, BANDS, MAX_BLOCKS], F32)
            planes = bands[:, :, :blocks].rearrange("c (s v) (i j) -> c s v i j", v=2, j=OUT_COLS)
            nc.vector.tensor_tensor(out=planes[:, :, 0, :, :], in0=top, in1=bottom, op=ADD)
            nc.vector.tensor_tensor(out=planes[:, :, 1, :, :], in0=top, in1=bottom, op=SUBTRACT)
            return bands

        def group(g, bands):
            blocks = chunks[g][2] * OUT_COLS
            grouped = work.tile([P, MAX_BLOCKS * BANDS], BF16, align_bytes=64)
            nc.scalar.mul(
                out=grouped[:, : blocks * BANDS].rearrange("c (m i t) -> c m t i", t=BANDS, i=4),
                in_=bands[:, :, :blocks].rearrange("c t (m i) -> c m t i", i=4),
                mul=0.5,
            )
            return grouped

        def group_on_vector(g, bands, grouped):
            blocks = vector_rows(g) * OUT_COLS
            nc.vector.tensor_scalar_mul(
                out=grouped[:, : blocks * BANDS].rearrange("c (m t) -> c m t", t=BANDS),
                in0=bands[:, :, :blocks].rearrange("c t m -> c m t"),
                scalar1=0.5,
            )

        def turn_pixels(parts):
            total = sum(rows for pixels, first, rows in parts)
            turned = psum_t.tile([P, total, P], BF16)
            u = 0
            for pixels, first, rows in parts:
                for i in range(first, first + rows):
                    nc.tensor.transpose(turned[:, u, :], pixels[:, ROW_PIXELS * i : ROW_PIXELS * (i + 1)], plus_one[:])
                    u += 1
            return turned

        def copy_turned(turned):
            turned_pixels = const.tile([P, MIXED_ROWS + 4, P], BF16)
            nc.scalar.copy(out=turned_pixels[:], in_=turned[:])
            return turned_pixels

        def haar_rows(turned_pixels, first, rows):
            made = psum_h.tile([P, 4, P], F32)
            for i in range(rows):
                nc.tensor.matmul(
                    out=made[:, i, :], lhsT=turned_pixels[:, first + i, :], rhs=haar[:], start=True, stop=True
                )
            return made

        def round_rows(made, rows, target):
            nc.scalar.mul(
                out=target.rearrange("c (i m) -> c i m", m=P), in_=made[:, :rows, :], mul=0.5
            )

        def finish(g, grouped):
            n, first, rows = chunks[g]
            blocks = rows * OUT_COLS
            codes = work.tile([P, MAX_BLOCKS], U32, align_bytes=64)
            scales = work.tile([P, MAX_BLOCKS], U8, align_bytes=64)
            nc.vector.quantize_mx(
                out=codes[:, :blocks].bitcast(FP8X4), scales=scales[:, :blocks], in_=grouped[:, : blocks * BANDS]
            )
            acc = psum.tile([P, MAX_BLOCKS], F32)
            nc.tensor.matmul_mx(
                out=acc[:, :blocks],
                lhsT=w_codes[:].bitcast(FP8X4),
                lhsT_scale=w_scales[:],
                rhs=codes[:, :blocks].bitcast(FP8X4),
                rhs_scale=scales[:, :blocks],
                start=True,
                stop=True,
            )
            result = results.tile([P, MAX_BLOCKS], F32)
            nc.scalar.copy(out=result[:, :blocks], in_=acc[:, :blocks])
            nc.sync.dma_start(
                out=out[n, :, first : first + rows, :].rearrange("o i j -> o (i j)"), in_=result[:, :blocks]
            )

        w_rows = const.tile([P, BANDS * P], BF16)
        chunk_pixels = []
        for g in range(count):
            if g == 3:
                nc.sync.dma_start(out=w_rows[:], in_=w_fusion.rearrange("o k a b -> o (k a b)"))
            if g == 0:
                chunk_pixels.append([load_first_half(0), load_first_half(1)])
            else:
                chunk_pixels.append(load_pixels(g))

        plus_one = const.tile([P, P], BF16)
        make_identity(nc, plus_one[:])
        identity = const.tile([P, P], F32)
        nc.scalar.copy(out=identity[:], in_=plus_one[:])
        haar = const.tile([P, P], BF16)
        sums = const.tile([P, 2, P // 2], BF16)
        pixel_pairs = plus_one[:].rearrange("q (m e) -> q m e", e=2)
        for s, op in enumerate((ADD, SUBTRACT)):
            nc.vector.tensor_tensor(out=sums[:, s, :], in0=pixel_pairs[:, :, 0], in1=pixel_pairs[:, :, 1], op=op)
        row_pairs = sums[:].rearrange("q s (r j) -> q s r j", r=2)
        bands_of = haar[:].rearrange("q (j s v) -> q s v j", s=2, v=2)
        for v, op in enumerate((ADD, SUBTRACT)):
            nc.vector.tensor_tensor(out=bands_of[:, :, v, :], in0=row_pairs[:, :, 0, :], in1=row_pairs[:, :, 1, :], op=op)
        w_grouped = const.tile([P, P * BANDS], BF16, align_bytes=64)
        w_codes = const.tile([P, P], U32, align_bytes=64)
        w_scales = const.tile([P, P], U8, align_bytes=64)

        def turn_weights():
            w_words = w_rows[:].bitcast(F32).rearrange("o (c u) -> o c u", u=2)
            w_turned = psum_w.tile([P, 2, P], F32)
            for u in range(2):
                nc.tensor.transpose(w_turned[:, u, :], w_words[:, :, u], identity[:])
            nc.scalar.copy(
                out=w_grouped[:].bitcast(F32).rearrange("c (o u) -> c o u", u=2),
                in_=w_turned[:].rearrange("c u o -> c o u"),
            )

        last = count - 2
        chunk_across = {}
        chunk_grouped = {}
        for g in range(-LAG - 1, last + 1):
            if g + LAG + 1 <= last:
                if g + LAG + 1 == 0:
                    chunk_across[0] = horizontal_first(chunk_pixels[0])
                else:
                    chunk_across[g + LAG + 1] = horizontal(g + LAG + 1, chunk_pixels[g + LAG + 1])
            if 0 <= g + LAG <= last:
                bands = vertical(g + LAG, chunk_across[g + LAG])
                if g + LAG < last:
                    chunk_grouped[g + LAG] = group(g + LAG, bands)
            if g == -1:
                turn_weights()
            if g == 0:
                nc.vector.quantize_mx(out=w_codes[:].bitcast(FP8X4), scales=w_scales[:], in_=w_grouped[:])
            if g >= 0:
                finish(g, chunk_grouped[g])
            if g == 0:
                turned = turn_pixels(((chunk_pixels[last], MIXED_ROWS, MIXED_ROWS), (chunk_pixels[last + 1], 0, 4)))
            if g == 1:
                turned_pixels = copy_turned(turned)
            if g == 2:
                made_mixed = haar_rows(turned_pixels, 0, MIXED_ROWS)
                made_last = haar_rows(turned_pixels, MIXED_ROWS, 4)
                half = MIXED_ROWS * OUT_COLS * BANDS
                for c in (last, last + 1):
                    chunk_grouped[c] = const.tile([P, 4 * OUT_COLS * BANDS], BF16, align_bytes=64, name="grouped%d" % c)
            if g == 3:
                round_rows(made_last, 4, chunk_grouped[last + 1][:])
            if g == 4:
                round_rows(made_mixed, MIXED_ROWS, chunk_grouped[last][:, half : 2 * half])
            if g == 5:
                finish(last + 1, chunk_grouped[last + 1])
            if g + LAG == last:
                group_on_vector(last, bands, chunk_grouped[last])
